import numpy as np
import ml_dtypes

BF16 = ml_dtypes.bfloat16


def bf(x):
    return np.asarray(x, np.float32).astype(BF16)


def f32(x):
    return np.asarray(x, np.float32)


def f64(x):
    return np.asarray(x).astype(np.float64)


def striped(idx):
    return np.tile(idx.reshape(-1, 16).T, (8, 1))


D, HALF, S, M, N, MAXPOS = 128, 64, 2048, 256, 1024, 1024
THETA = 10000.0


def setup_inputs():
    inv_freq = 1.0 / THETA ** (np.arange(HALF) / HALF)
    ang = np.outer(inv_freq, np.random.uniform(0.0, MAXPOS, N))
    ang = np.concatenate([ang, ang], axis=0)
    return {"x": bf(np.random.standard_normal((D, S))), "w": bf(np.random.standard_normal((D, M)) / np.sqrt(D)), "cos": f32(np.cos(ang)), "sin": f32(np.sin(ang)), "offs": striped(np.random.permutation(S)[:N])}


def reference(x, w, cos, sin, offs):
    idx = offs[:16].T.reshape(-1)
    p = f64(w).T @ f64(x)[:, idx]
    key, val = p[:D], p[D:]
    rot = np.concatenate([-key[HALF:], key[:HALF]], axis=0)
    return np.concatenate([key * f64(cos) + rot * f64(sin), val], axis=0)

@@ -1,0 +1,58 @@
+import concourse.mybir as mybir
+
+BF16, F32, U16 = mybir.dt.bfloat16, mybir.dt.float32, mybir.dt.uint16
+MULT, ADD = mybir.AluOpType.mult, mybir.AluOpType.add
+
+D = 128
+HALF = D // 2
+S = 2048
+N = 1024
+PIECE = 512
+
+FLOPS = 2 * D * (2 * D) * N
+
+
+def tile_unpaddedllamaattention_kernel(tc, x, w, cos, sin, offs, out):
+    nc = tc.nc
+    with (
+        tc.tile_pool(name="held", bufs=1) as held,
+        tc.tile_pool(name="work", bufs=2) as work,
+        tc.psum_pool(name="psum", bufs=2) as psum,
+    ):
+        offsets = held.tile([D, N // 16], U16, name="offsets")
+        nc.sync.dma_start(offsets[:], offs)
+        w_sb = held.tile([D, 2 * D], BF16, name="w_sb")
+        nc.sync.dma_start(w_sb[:], w)
+        x_sb = held.tile([D, S], BF16, name="x_sb")
+        nc.sync.dma_start(x_sb[:], x)
+        cos_sb = held.tile([D, N], F32, name="cos_sb")
+        nc.sync.dma_start(cos_sb[:], cos)
+        sin_sb = held.tile([D, N], F32, name="sin_sb")
+        nc.sync.dma_start(sin_sb[:], sin)
+
+        w_rot = held.tile([D, D], BF16, name="w_rot")
+        nc.vector.tensor_scalar_mul(w_rot[:, 0:HALF], w_sb[:, HALF:D], -1.0)
+        nc.vector.tensor_copy(w_rot[:, HALF:D], w_sb[:, 0:HALF])
+
+        for piece in range(N // PIECE):
+            cols = slice(piece * PIECE, (piece + 1) * PIECE)
+            picked = x_sb[:].indirect(offsets[:, piece * (PIECE // 16) : (piece + 1) * (PIECE // 16)])
+
+            key = psum.tile([D, PIECE], F32, name="key")
+            nc.tensor.matmul(key[:], w_sb[:, 0:D], picked, start=True, stop=True)
+            partner = psum.tile([D, PIECE], F32, name="partner")
+            nc.tensor.matmul(partner[:], w_rot[:], picked, start=True, stop=True)
+            val = psum.tile([D, PIECE], F32, name="val")
+            nc.tensor.matmul(val[:], w_sb[:, D : 2 * D], picked, start=True, stop=True)
+
+            key_cos = work.tile([D, PIECE], F32, name="key_cos")
+            nc.vector.tensor_tensor(key_cos[:], key[:], cos_sb[:, cols], MULT)
+            partner_sin = work.tile([D, PIECE], F32, name="partner_sin")
+            nc.vector.tensor_tensor(partner_sin[:], partner[:], sin_sb[:, cols], MULT)
+            rotated = work.tile([D, PIECE], F32, name="rotated")
+            nc.vector.tensor_tensor(rotated[:], key_cos[:], partner_sin[:], ADD)
+            nc.sync.dma_start(out[0:D, cols], rotated[:])
+
+            val_sb = work.tile([D, PIECE], F32, name="val_sb")
+            nc.scalar.copy(val_sb[:], val[:])
+            nc.scalar.dma_start(out[D : 2 * D, cols], val_sb[:])

@@ -8,6 +8,7 @@ HALF = D // 2
 S = 2048
 N = 1024
 PIECE = 512
+PIECES = N // PIECE
 
 FLOPS = 2 * D * (2 * D) * N
 
@@ -16,34 +17,35 @@ def tile_unpaddedllamaattention_kernel(tc, x, w, cos, sin, offs, out):
     nc = tc.nc
     with (
         tc.tile_pool(name="held", bufs=1) as held,
-        tc.tile_pool(name="work", bufs=2) as work,
-        tc.psum_pool(name="psum", bufs=2) as psum,
+        tc.tile_pool(name="work", bufs=PIECES) as work,
+        tc.psum_pool(name="psum", bufs=PIECES) as psum,
     ):
         offsets = held.tile([D, N // 16], U16, name="offsets")
         nc.sync.dma_start(offsets[:], offs)
-        w_sb = held.tile([D, 2 * D], BF16, name="w_sb")
-        nc.sync.dma_start(w_sb[:], w)
         x_sb = held.tile([D, S], BF16, name="x_sb")
         nc.sync.dma_start(x_sb[:], x)
+        w_sb = held.tile([D, 2 * D], BF16, name="w_sb")
+        nc.scalar.dma_start(w_sb[:], w)
         cos_sb = held.tile([D, N], F32, name="cos_sb")
-        nc.sync.dma_start(cos_sb[:], cos)
         sin_sb = held.tile([D, N], F32, name="sin_sb")
-        nc.sync.dma_start(sin_sb[:], sin)
+        for piece in range(PIECES):
+            cols = slice(piece * PIECE, (piece + 1) * PIECE)
+            nc.sync.dma_start(cos_sb[:, cols], cos[:, cols])
+            nc.sync.dma_start(sin_sb[:, cols], sin[:, cols])
 
         w_rot = held.tile([D, D], BF16, name="w_rot")
         nc.vector.tensor_scalar_mul(w_rot[:, 0:HALF], w_sb[:, HALF:D], -1.0)
         nc.vector.tensor_copy(w_rot[:, HALF:D], w_sb[:, 0:HALF])
 
-        for piece in range(N // PIECE):
-            cols = slice(piece * PIECE, (piece + 1) * PIECE)
-            picked = x_sb[:].indirect(offsets[:, piece * (PIECE // 16) : (piece + 1) * (PIECE // 16)])
+        def picked(piece):
+            return x_sb[:].indirect(offsets[:, piece * (PIECE // 16) : (piece + 1) * (PIECE // 16)])
 
+        for piece in range(PIECES):
+            cols = slice(piece * PIECE, (piece + 1) * PIECE)
             key = psum.tile([D, PIECE], F32, name="key")
-            nc.tensor.matmul(key[:], w_sb[:, 0:D], picked, start=True, stop=True)
+            nc.tensor.matmul(key[:], w_sb[:, 0:D], picked(piece), start=True, stop=True)
             partner = psum.tile([D, PIECE], F32, name="partner")
-            nc.tensor.matmul(partner[:], w_rot[:], picked, start=True, stop=True)
-            val = psum.tile([D, PIECE], F32, name="val")
-            nc.tensor.matmul(val[:], w_sb[:, D : 2 * D], picked, start=True, stop=True)
+            nc.tensor.matmul(partner[:], w_rot[:], picked(piece), start=True, stop=True)
 
             key_cos = work.tile([D, PIECE], F32, name="key_cos")
             nc.vector.tensor_tensor(key_cos[:], key[:], cos_sb[:, cols], MULT)
@@ -53,6 +55,10 @@ def tile_unpaddedllamaattention_kernel(tc, x, w, cos, sin, offs, out):
             nc.vector.tensor_tensor(rotated[:], key_cos[:], partner_sin[:], ADD)
             nc.sync.dma_start(out[0:D, cols], rotated[:])
 
+        for piece in range(PIECES):
+            cols = slice(piece * PIECE, (piece + 1) * PIECE)
+            val = psum.tile([D, PIECE], F32, name="val")
+            nc.tensor.matmul(val[:], w_sb[:, D : 2 * D], picked(piece), start=True, stop=True)
             val_sb = work.tile([D, PIECE], F32, name="val_sb")
             nc.scalar.copy(val_sb[:], val[:])
             nc.scalar.dma_start(out[D : 2 * D, cols], val_sb[:])

@@ -9,6 +9,8 @@ S = 2048
 N = 1024
 PIECE = 512
 PIECES = N // PIECE
+CHUNK = 256
+CHUNKS = N // CHUNK
 
 FLOPS = 2 * D * (2 * D) * N
 
@@ -17,7 +19,7 @@ def tile_unpaddedllamaattention_kernel(tc, x, w, cos, sin, offs, out):
     nc = tc.nc
     with (
         tc.tile_pool(name="held", bufs=1) as held,
-        tc.tile_pool(name="work", bufs=PIECES) as work,
+        tc.tile_pool(name="work", bufs=CHUNKS) as work,
         tc.psum_pool(name="psum", bufs=PIECES) as psum,
     ):
         offsets = held.tile([D, N // 16], U16, name="offsets")
@@ -41,19 +43,22 @@ def tile_unpaddedllamaattention_kernel(tc, x, w, cos, sin, offs, out):
             return x_sb[:].indirect(offsets[:, piece * (PIECE // 16) : (piece + 1) * (PIECE // 16)])
 
         for piece in range(PIECES):
-            cols = slice(piece * PIECE, (piece + 1) * PIECE)
             key = psum.tile([D, PIECE], F32, name="key")
             nc.tensor.matmul(key[:], w_sb[:, 0:D], picked(piece), start=True, stop=True)
             partner = psum.tile([D, PIECE], F32, name="partner")
             nc.tensor.matmul(partner[:], w_rot[:], picked(piece), start=True, stop=True)
 
-            key_cos = work.tile([D, PIECE], F32, name="key_cos")
-            nc.vector.tensor_tensor(key_cos[:], key[:], cos_sb[:, cols], MULT)
-            partner_sin = work.tile([D, PIECE], F32, name="partner_sin")
-            nc.vector.tensor_tensor(partner_sin[:], partner[:], sin_sb[:, cols], MULT)
-            rotated = work.tile([D, PIECE], F32, name="rotated")
-            nc.vector.tensor_tensor(rotated[:], key_cos[:], partner_sin[:], ADD)
-            nc.sync.dma_start(out[0:D, cols], rotated[:])
+            for chunk in range(piece * PIECE // CHUNK, (piece + 1) * PIECE // CHUNK):
+                cols = slice(chunk * CHUNK, (chunk + 1) * CHUNK)
+                in_piece = slice(chunk * CHUNK - piece * PIECE, (chunk + 1) * CHUNK - piece * PIECE)
+                key_cos = work.tile([D, CHUNK], F32, name="key_cos")
+                nc.vector.tensor_tensor(key_cos[:], key[:, in_piece], cos_sb[:, cols], MULT)
+                partner_sin = work.tile([D, CHUNK], F32, name="partner_sin")
+                nc.vector.tensor_tensor(partner_sin[:], partner[:, in_piece], sin_sb[:, cols], MULT)
+                adder = nc.vector if chunk == CHUNKS - 1 else nc.gpsimd
+                rotated = work.tile([D, CHUNK], F32, name="rotated")
+                adder.tensor_tensor(rotated[:], key_cos[:], partner_sin[:], ADD)
+                nc.sync.dma_start(out[0:D, cols], rotated[:])
 
         for piece in range(PIECES):
             cols = slice(piece * PIECE, (piece + 1) * PIECE)

@@ -11,6 +11,7 @@ PIECE = 512
 PIECES = N // PIECE
 CHUNK = 256
 CHUNKS = N // CHUNK
+WARM_UPS = 6
 
 FLOPS = 2 * D * (2 * D) * N
 
@@ -21,6 +22,7 @@ def tile_unpaddedllamaattention_kernel(tc, x, w, cos, sin, offs, out):
         tc.tile_pool(name="held", bufs=1) as held,
         tc.tile_pool(name="work", bufs=CHUNKS) as work,
         tc.psum_pool(name="psum", bufs=PIECES) as psum,
+        tc.psum_pool(name="idle", bufs=1) as idle,
     ):
         offsets = held.tile([D, N // 16], U16, name="offsets")
         nc.sync.dma_start(offsets[:], offs)
@@ -38,6 +40,12 @@ def tile_unpaddedllamaattention_kernel(tc, x, w, cos, sin, offs, out):
         w_rot = held.tile([D, D], BF16, name="w_rot")
         nc.vector.tensor_scalar_mul(w_rot[:, 0:HALF], w_sb[:, HALF:D], -1.0)
         nc.vector.tensor_copy(w_rot[:, HALF:D], w_sb[:, 0:HALF])
+
+        zeros = held.tile([D, PIECE], BF16, name="zeros")
+        nc.gpsimd.memset(zeros[:], 0.0)
+        unread = idle.tile([D, PIECE], F32, name="unread")
+        for warm_up in range(WARM_UPS):
+            nc.tensor.matmul(unread[:], zeros[:, 0:D], zeros[:], start=True, stop=True)
 
         def picked(piece):
             return x_sb[:].indirect(offsets[:, piece * (PIECE // 16) : (piece + 1) * (PIECE // 16)])

@@ -11,7 +11,6 @@ PIECE = 512
 PIECES = N // PIECE
 CHUNK = 256
 CHUNKS = N // CHUNK
-WARM_UPS = 6
 
 FLOPS = 2 * D * (2 * D) * N
 
@@ -22,7 +21,6 @@ def tile_unpaddedllamaattention_kernel(tc, x, w, cos, sin, offs, out):
         tc.tile_pool(name="held", bufs=1) as held,
         tc.tile_pool(name="work", bufs=CHUNKS) as work,
         tc.psum_pool(name="psum", bufs=PIECES) as psum,
-        tc.psum_pool(name="idle", bufs=1) as idle,
     ):
         offsets = held.tile([D, N // 16], U16, name="offsets")
         nc.sync.dma_start(offsets[:], offs)
@@ -41,14 +39,16 @@ def tile_unpaddedllamaattention_kernel(tc, x, w, cos, sin, offs, out):
         nc.vector.tensor_scalar_mul(w_rot[:, 0:HALF], w_sb[:, HALF:D], -1.0)
         nc.vector.tensor_copy(w_rot[:, HALF:D], w_sb[:, 0:HALF])
 
-        zeros = held.tile([D, PIECE], BF16, name="zeros")
-        nc.gpsimd.memset(zeros[:], 0.0)
-        unread = idle.tile([D, PIECE], F32, name="unread")
-        for warm_up in range(WARM_UPS):
-            nc.tensor.matmul(unread[:], zeros[:, 0:D], zeros[:], start=True, stop=True)
-
         def picked(piece):
             return x_sb[:].indirect(offsets[:, piece * (PIECE // 16) : (piece + 1) * (PIECE // 16)])
+
+        for piece in range(PIECES):
+            cols = slice(piece * PIECE, (piece + 1) * PIECE)
+            val = psum.tile([D, PIECE], F32, name="val")
+            nc.tensor.matmul(val[:], w_sb[:, D : 2 * D], picked(piece), start=True, stop=True)
+            val_sb = work.tile([D, PIECE], F32, name="val_sb")
+            nc.scalar.copy(val_sb[:], val[:])
+            nc.scalar.dma_start(out[D : 2 * D, cols], val_sb[:])
 
         for piece in range(PIECES):
             key = psum.tile([D, PIECE], F32, name="key")
@@ -67,11 +67,3 @@ def tile_unpaddedllamaattention_kernel(tc, x, w, cos, sin, offs, out):
                 rotated = work.tile([D, CHUNK], F32, name="rotated")
                 adder.tensor_tensor(rotated[:], key_cos[:], partner_sin[:], ADD)
                 nc.sync.dma_start(out[0:D, cols], rotated[:])
-
-        for piece in range(PIECES):
-            cols = slice(piece * PIECE, (piece + 1) * PIECE)
-            val = psum.tile([D, PIECE], F32, name="val")
-            nc.tensor.matmul(val[:], w_sb[:, D : 2 * D], picked(piece), start=True, stop=True)
-            val_sb = work.tile([D, PIECE], F32, name="val_sb")
-            nc.scalar.copy(val_sb[:], val[:])
-            nc.scalar.dma_start(out[D : 2 * D, cols], val_sb[:])

@@ -24,16 +24,16 @@ def tile_unpaddedllamaattention_kernel(tc, x, w, cos, sin, offs, out):
     ):
         offsets = held.tile([D, N // 16], U16, name="offsets")
         nc.sync.dma_start(offsets[:], offs)
-        x_sb = held.tile([D, S], BF16, name="x_sb")
-        nc.sync.dma_start(x_sb[:], x)
         w_sb = held.tile([D, 2 * D], BF16, name="w_sb")
-        nc.scalar.dma_start(w_sb[:], w)
+        nc.sync.dma_start(w_sb[:], w)
+        x_sb = held.tile([D, S], BF16, name="x_sb")
+        nc.scalar.dma_start(x_sb[:], x)
         cos_sb = held.tile([D, N], F32, name="cos_sb")
         sin_sb = held.tile([D, N], F32, name="sin_sb")
         for piece in range(PIECES):
             cols = slice(piece * PIECE, (piece + 1) * PIECE)
-            nc.sync.dma_start(cos_sb[:, cols], cos[:, cols])
-            nc.sync.dma_start(sin_sb[:, cols], sin[:, cols])
+            nc.scalar.dma_start(cos_sb[:, cols], cos[:, cols])
+            nc.scalar.dma_start(sin_sb[:, cols], sin[:, cols])
 
         w_rot = held.tile([D, D], BF16, name="w_rot")
         nc.vector.tensor_scalar_mul(w_rot[:, 0:HALF], w_sb[:, HALF:D], -1.0)
@@ -41,14 +41,6 @@ def tile_unpaddedllamaattention_kernel(tc, x, w, cos, sin, offs, out):
 
         def picked(piece):
             return x_sb[:].indirect(offsets[:, piece * (PIECE // 16) : (piece + 1) * (PIECE // 16)])
-
-        for piece in range(PIECES):
-            cols = slice(piece * PIECE, (piece + 1) * PIECE)
-            val = psum.tile([D, PIECE], F32, name="val")
-            nc.tensor.matmul(val[:], w_sb[:, D : 2 * D], picked(piece), start=True, stop=True)
-            val_sb = work.tile([D, PIECE], F32, name="val_sb")
-            nc.scalar.copy(val_sb[:], val[:])
-            nc.scalar.dma_start(out[D : 2 * D, cols], val_sb[:])
 
         for piece in range(PIECES):
             key = psum.tile([D, PIECE], F32, name="key")
@@ -67,3 +59,11 @@ def tile_unpaddedllamaattention_kernel(tc, x, w, cos, sin, offs, out):
                 rotated = work.tile([D, CHUNK], F32, name="rotated")
                 adder.tensor_tensor(rotated[:], key_cos[:], partner_sin[:], ADD)
                 nc.sync.dma_start(out[0:D, cols], rotated[:])
+
+        for piece in range(PIECES):
+            cols = slice(piece * PIECE, (piece + 1) * PIECE)
+            val = psum.tile([D, PIECE], F32, name="val")
+            nc.tensor.matmul(val[:], w_sb[:, D : 2 * D], picked(piece), start=True, stop=True)
+            val_sb = work.tile([D, PIECE], F32, name="val_sb")
+            nc.scalar.copy(val_sb[:], val[:])
+            nc.scalar.dma_start(out[D : 2 * D, cols], val_sb[:])

@@ -61,9 +61,11 @@ def tile_unpaddedllamaattention_kernel(tc, x, w, cos, sin, offs, out):
                 nc.sync.dma_start(out[0:D, cols], rotated[:])
 
         for piece in range(PIECES):
-            cols = slice(piece * PIECE, (piece + 1) * PIECE)
             val = psum.tile([D, PIECE], F32, name="val")
             nc.tensor.matmul(val[:], w_sb[:, D : 2 * D], picked(piece), start=True, stop=True)
-            val_sb = work.tile([D, PIECE], F32, name="val_sb")
-            nc.scalar.copy(val_sb[:], val[:])
-            nc.scalar.dma_start(out[D : 2 * D, cols], val_sb[:])
+            for chunk in range(piece * PIECE // CHUNK, (piece + 1) * PIECE // CHUNK):
+                cols = slice(chunk * CHUNK, (chunk + 1) * CHUNK)
+                in_piece = slice(chunk * CHUNK - piece * PIECE, (chunk + 1) * CHUNK - piece * PIECE)
+                val_sb = work.tile([D, CHUNK], F32, name="val_sb")
+                nc.scalar.copy(val_sb[:], val[:, in_piece])
+                nc.scalar.dma_start(out[D : 2 * D, cols], val_sb[:])

@@ -20,7 +20,7 @@ def tile_unpaddedllamaattention_kernel(tc, x, w, cos, sin, offs, out):
     with (
         tc.tile_pool(name="held", bufs=1) as held,
         tc.tile_pool(name="work", bufs=CHUNKS) as work,
-        tc.psum_pool(name="psum", bufs=PIECES) as psum,
+        tc.psum_pool(name="psum", bufs=2) as psum,
     ):
         offsets = held.tile([D, N // 16], U16, name="offsets")
         nc.sync.dma_start(offsets[:], offs)
@@ -39,33 +39,25 @@ def tile_unpaddedllamaattention_kernel(tc, x, w, cos, sin, offs, out):
         nc.vector.tensor_scalar_mul(w_rot[:, 0:HALF], w_sb[:, HALF:D], -1.0)
         nc.vector.tensor_copy(w_rot[:, HALF:D], w_sb[:, 0:HALF])
 
-        def picked(piece):
-            return x_sb[:].indirect(offsets[:, piece * (PIECE // 16) : (piece + 1) * (PIECE // 16)])
+        for chunk in range(CHUNKS):
+            cols = slice(chunk * CHUNK, (chunk + 1) * CHUNK)
+            picked = x_sb[:].indirect(offsets[:, chunk * (CHUNK // 16) : (chunk + 1) * (CHUNK // 16)])
+            key = psum.tile([D, CHUNK], F32, name="key")
+            nc.tensor.matmul(key[:], w_sb[:, 0:D], picked, start=True, stop=True)
+            partner = psum.tile([D, CHUNK], F32, name="partner")
+            nc.tensor.matmul(partner[:], w_rot[:], picked, start=True, stop=True)
+            val = psum.tile([D, CHUNK], F32, name="val")
+            nc.tensor.matmul(val[:], w_sb[:, D : 2 * D], picked, start=True, stop=True)
 
-        for piece in range(PIECES):
-            key = psum.tile([D, PIECE], F32, name="key")
-            nc.tensor.matmul(key[:], w_sb[:, 0:D], picked(piece), start=True, stop=True)
-            partner = psum.tile([D, PIECE], F32, name="partner")
-            nc.tensor.matmul(partner[:], w_rot[:], picked(piece), start=True, stop=True)
+            key_cos = work.tile([D, CHUNK], F32, name="key_cos")
+            nc.vector.tensor_tensor(key_cos[:], key[:], cos_sb[:, cols], MULT)
+            partner_sin = work.tile([D, CHUNK], F32, name="partner_sin")
+            nc.vector.tensor_tensor(partner_sin[:], partner[:], sin_sb[:, cols], MULT)
+            adder = nc.vector if chunk == CHUNKS - 1 else nc.gpsimd
+            rotated = work.tile([D, CHUNK], F32, name="rotated")
+            adder.tensor_tensor(rotated[:], key_cos[:], partner_sin[:], ADD)
+            nc.sync.dma_start(out[0:D, cols], rotated[:])
 
-            for chunk in range(piece * PIECE // CHUNK, (piece + 1) * PIECE // CHUNK):
-                cols = slice(chunk * CHUNK, (chunk + 1) * CHUNK)
-                in_piece = slice(chunk * CHUNK - piece * PIECE, (chunk + 1) * CHUNK - piece * PIECE)
-                key_cos = work.tile([D, CHUNK], F32, name="key_cos")
-                nc.vector.tensor_tensor(key_cos[:], key[:, in_piece], cos_sb[:, cols], MULT)
-                partner_sin = work.tile([D, CHUNK], F32, name="partner_sin")
-                nc.vector.tensor_tensor(partner_sin[:], partner[:, in_piece], sin_sb[:, cols], MULT)
-                adder = nc.vector if chunk == CHUNKS - 1 else nc.gpsimd
-                rotated = work.tile([D, CHUNK], F32, name="rotated")
-                adder.tensor_tensor(rotated[:], key_cos[:], partner_sin[:], ADD)
-                nc.sync.dma_start(out[0:D, cols], rotated[:])
-
-        for piece in range(PIECES):
-            val = psum.tile([D, PIECE], F32, name="val")
-            nc.tensor.matmul(val[:], w_sb[:, D : 2 * D], picked(piece), start=True, stop=True)
-            for chunk in range(piece * PIECE // CHUNK, (piece + 1) * PIECE // CHUNK):
-                cols = slice(chunk * CHUNK, (chunk + 1) * CHUNK)
-                in_piece = slice(chunk * CHUNK - piece * PIECE, (chunk + 1) * CHUNK - piece * PIECE)
-                val_sb = work.tile([D, CHUNK], F32, name="val_sb")
-                nc.scalar.copy(val_sb[:], val[:, in_piece])
-                nc.scalar.dma_start(out[D : 2 * D, cols], val_sb[:])
+            val_sb = work.tile([D, CHUNK], F32, name="val_sb")
+            nc.scalar.copy(val_sb[:], val[:])
+            nc.scalar.dma_start(out[D : 2 * D, cols], val_sb[:])

@@ -53,7 +53,7 @@ def tile_unpaddedllamaattention_kernel(tc, x, w, cos, sin, offs, out):
             nc.vector.tensor_tensor(key_cos[:], key[:], cos_sb[:, cols], MULT)
             partner_sin = work.tile([D, CHUNK], F32, name="partner_sin")
             nc.vector.tensor_tensor(partner_sin[:], partner[:], sin_sb[:, cols], MULT)
-            adder = nc.vector if chunk == CHUNKS - 1 else nc.gpsimd
+            adder = nc.gpsimd if chunk < CHUNKS // 2 else nc.vector
             rotated = work.tile([D, CHUNK], F32, name="rotated")
             adder.tensor_tensor(rotated[:], key_cos[:], partner_sin[:], ADD)
             nc.sync.dma_start(out[0:D, cols], rotated[:])

@@ -8,7 +8,6 @@ HALF = D // 2
 S = 2048
 N = 1024
 PIECE = 512
-PIECES = N // PIECE
 CHUNK = 256
 CHUNKS = N // CHUNK
 
@@ -30,10 +29,11 @@ def tile_unpaddedllamaattention_kernel(tc, x, w, cos, sin, offs, out):
         nc.scalar.dma_start(x_sb[:], x)
         cos_sb = held.tile([D, N], F32, name="cos_sb")
         sin_sb = held.tile([D, N], F32, name="sin_sb")
-        for piece in range(PIECES):
-            cols = slice(piece * PIECE, (piece + 1) * PIECE)
-            nc.scalar.dma_start(cos_sb[:, cols], cos[:, cols])
-            nc.scalar.dma_start(sin_sb[:, cols], sin[:, cols])
+        nc.scalar.dma_start(cos_sb[:, 0:PIECE], cos[:, 0:PIECE])
+        nc.scalar.dma_start(sin_sb[:, 0:PIECE], sin[:, 0:PIECE])
+        nc.scalar.dma_start(cos_sb[:, PIECE:N], cos[:, PIECE:N])
+        for first in (PIECE, PIECE + CHUNK):
+            nc.scalar.dma_start(sin_sb[:, first : first + CHUNK], sin[:, first : first + CHUNK])
 
         w_rot = held.tile([D, D], BF16, name="w_rot")
         nc.vector.tensor_scalar_mul(w_rot[:, 0:HALF], w_sb[:, HALF:D], -1.0)

@@ -8,8 +8,8 @@ HALF = D // 2
 S = 2048
 N = 1024
 PIECE = 512
+PIECES = N // PIECE
 CHUNK = 256
-CHUNKS = N // CHUNK
 
 FLOPS = 2 * D * (2 * D) * N
 
@@ -18,7 +18,7 @@ def tile_unpaddedllamaattention_kernel(tc, x, w, cos, sin, offs, out):
     nc = tc.nc
     with (
         tc.tile_pool(name="held", bufs=1) as held,
-        tc.tile_pool(name="work", bufs=CHUNKS) as work,
+        tc.tile_pool(name="work", bufs=N // CHUNK) as work,
         tc.psum_pool(name="psum", bufs=2) as psum,
     ):
         offsets = held.tile([D, N // 16], U16, name="offsets")
@@ -39,25 +39,30 @@ def tile_unpaddedllamaattention_kernel(tc, x, w, cos, sin, offs, out):
         nc.vector.tensor_scalar_mul(w_rot[:, 0:HALF], w_sb[:, HALF:D], -1.0)
         nc.vector.tensor_copy(w_rot[:, HALF:D], w_sb[:, 0:HALF])
 
-        for chunk in range(CHUNKS):
-            cols = slice(chunk * CHUNK, (chunk + 1) * CHUNK)
-            picked = x_sb[:].indirect(offsets[:, chunk * (CHUNK // 16) : (chunk + 1) * (CHUNK // 16)])
-            key = psum.tile([D, CHUNK], F32, name="key")
-            nc.tensor.matmul(key[:], w_sb[:, 0:D], picked, start=True, stop=True)
-            partner = psum.tile([D, CHUNK], F32, name="partner")
-            nc.tensor.matmul(partner[:], w_rot[:], picked, start=True, stop=True)
-            val = psum.tile([D, CHUNK], F32, name="val")
-            nc.tensor.matmul(val[:], w_sb[:, D : 2 * D], picked, start=True, stop=True)
+        def project(weights, first, count, name):
+            product = psum.tile([D, count], F32, name=name)
+            picked = x_sb[:].indirect(offsets[:, first // 16 : (first + count) // 16])
+            nc.tensor.matmul(product[:], weights, picked, start=True, stop=True)
+            return product
 
-            key_cos = work.tile([D, CHUNK], F32, name="key_cos")
-            nc.vector.tensor_tensor(key_cos[:], key[:], cos_sb[:, cols], MULT)
-            partner_sin = work.tile([D, CHUNK], F32, name="partner_sin")
-            nc.vector.tensor_tensor(partner_sin[:], partner[:], sin_sb[:, cols], MULT)
-            adder = nc.gpsimd if chunk < CHUNKS // 2 else nc.vector
-            rotated = work.tile([D, CHUNK], F32, name="rotated")
-            adder.tensor_tensor(rotated[:], key_cos[:], partner_sin[:], ADD)
-            nc.sync.dma_start(out[0:D, cols], rotated[:])
+        for piece in range(PIECES):
+            chunks = (piece * PIECE, piece * PIECE + CHUNK)
+            key = project(w_sb[:, 0:D], piece * PIECE, PIECE, "key")
+            partners = [project(w_rot[:], first, CHUNK, "partner") for first in chunks]
+            vals = [project(w_sb[:, D : 2 * D], first, CHUNK, "val") for first in chunks]
+            key_cos = work.tile([D, PIECE], F32, name="key_cos")
+            nc.vector.tensor_tensor(key_cos[:], key[:], cos_sb[:, piece * PIECE : (piece + 1) * PIECE], MULT)
 
-            val_sb = work.tile([D, CHUNK], F32, name="val_sb")
-            nc.scalar.copy(val_sb[:], val[:])
-            nc.scalar.dma_start(out[D : 2 * D, cols], val_sb[:])
+            for first, partner, val in zip(chunks, partners, vals):
+                cols = slice(first, first + CHUNK)
+                in_piece = slice(first - piece * PIECE, first - piece * PIECE + CHUNK)
+                partner_sin = work.tile([D, CHUNK], F32, name="partner_sin")
+                nc.vector.tensor_tensor(partner_sin[:], partner[:], sin_sb[:, cols], MULT)
+                adder = nc.gpsimd if piece == 0 else nc.vector
+                rotated = work.tile([D, CHUNK], F32, name="rotated")
+                adder.tensor_tensor(rotated[:], key_cos[:, in_piece], partner_sin[:], ADD)
+                nc.sync.dma_start(out[0:D, cols], rotated[:])
+
+                val_sb = work.tile([D, CHUNK], F32, name="val_sb")
+                nc.scalar.copy(val_sb[:], val[:])
+                nc.scalar.dma_start(out[D : 2 * D, cols], val_sb[:])

@@ -48,8 +48,14 @@ def tile_unpaddedllamaattention_kernel(tc, x, w, cos, sin, offs, out):
         for piece in range(PIECES):
             chunks = (piece * PIECE, piece * PIECE + CHUNK)
             key = project(w_sb[:, 0:D], piece * PIECE, PIECE, "key")
-            partners = [project(w_rot[:], first, CHUNK, "partner") for first in chunks]
-            vals = [project(w_sb[:, D : 2 * D], first, CHUNK, "val") for first in chunks]
+            if piece < PIECES - 1:
+                partner = project(w_rot[:], piece * PIECE, PIECE, "partner")
+                val = project(w_sb[:, D : 2 * D], piece * PIECE, PIECE, "val")
+                partners = [partner[:, 0:CHUNK], partner[:, CHUNK:PIECE]]
+                vals = [val[:, 0:CHUNK], val[:, CHUNK:PIECE]]
+            else:
+                partners = [project(w_rot[:], first, CHUNK, "partner")[:] for first in chunks]
+                vals = [project(w_sb[:, D : 2 * D], first, CHUNK, "val")[:] for first in chunks]
             key_cos = work.tile([D, PIECE], F32, name="key_cos")
             nc.vector.tensor_tensor(key_cos[:], key[:], cos_sb[:, piece * PIECE : (piece + 1) * PIECE], MULT)
 
@@ -57,12 +63,12 @@ def tile_unpaddedllamaattention_kernel(tc, x, w, cos, sin, offs, out):
                 cols = slice(first, first + CHUNK)
                 in_piece = slice(first - piece * PIECE, first - piece * PIECE + CHUNK)
                 partner_sin = work.tile([D, CHUNK], F32, name="partner_sin")
-                nc.vector.tensor_tensor(partner_sin[:], partner[:], sin_sb[:, cols], MULT)
+                nc.vector.tensor_tensor(partner_sin[:], partner, sin_sb[:, cols], MULT)
                 adder = nc.gpsimd if piece == 0 else nc.vector
                 rotated = work.tile([D, CHUNK], F32, name="rotated")
                 adder.tensor_tensor(rotated[:], key_cos[:, in_piece], partner_sin[:], ADD)
                 nc.sync.dma_start(out[0:D, cols], rotated[:])
 
                 val_sb = work.tile([D, CHUNK], F32, name="val_sb")
-                nc.scalar.copy(val_sb[:], val[:])
+                nc.scalar.copy(val_sb[:], val)
                 nc.scalar.dma_start(out[D : 2 * D, cols], val_sb[:])

@@ -21,10 +21,10 @@ def tile_unpaddedllamaattention_kernel(tc, x, w, cos, sin, offs, out):
         tc.tile_pool(name="work", bufs=N // CHUNK) as work,
         tc.psum_pool(name="psum", bufs=2) as psum,
     ):
-        offsets = held.tile([D, N // 16], U16, name="offsets")
-        nc.sync.dma_start(offsets[:], offs)
         w_sb = held.tile([D, 2 * D], BF16, name="w_sb")
         nc.sync.dma_start(w_sb[:], w)
+        offsets = held.tile([D, N // 16], U16, name="offsets")
+        nc.sync.dma_start(offsets[:], offs)
         x_sb = held.tile([D, S], BF16, name="x_sb")
         nc.scalar.dma_start(x_sb[:], x)
         cos_sb = held.tile([D, N], F32, name="cos_sb")

import concourse.mybir as mybir

BF16, F32, U16 = mybir.dt.bfloat16, mybir.dt.float32, mybir.dt.uint16
MULT, ADD = mybir.AluOpType.mult, mybir.AluOpType.add

D = 128
HALF = D // 2
S = 2048
N = 1024
PIECE = 512
PIECES = N // PIECE
CHUNK = 256

FLOPS = 2 * D * (2 * D) * N


def tile_unpaddedllamaattention_kernel(tc, x, w, cos, sin, offs, out):
    nc = tc.nc
    with (
        tc.tile_pool(name="held", bufs=1) as held,
        tc.tile_pool(name="work", bufs=N // CHUNK) as work,
        tc.psum_pool(name="psum", bufs=2) as psum,
    ):
        w_sb = held.tile([D, 2 * D], BF16, name="w_sb")
        nc.sync.dma_start(w_sb[:], w)
        offsets = held.tile([D, N // 16], U16, name="offsets")
        nc.sync.dma_start(offsets[:], offs)
        x_sb = held.tile([D, S], BF16, name="x_sb")
        nc.scalar.dma_start(x_sb[:], x)
        cos_sb = held.tile([D, N], F32, name="cos_sb")
        sin_sb = held.tile([D, N], F32, name="sin_sb")
        nc.scalar.dma_start(cos_sb[:, 0:PIECE], cos[:, 0:PIECE])
        nc.scalar.dma_start(sin_sb[:, 0:PIECE], sin[:, 0:PIECE])
        nc.scalar.dma_start(cos_sb[:, PIECE:N], cos[:, PIECE:N])
        for first in (PIECE, PIECE + CHUNK):
            nc.scalar.dma_start(sin_sb[:, first : first + CHUNK], sin[:, first : first + CHUNK])

        w_rot = held.tile([D, D], BF16, name="w_rot")
        nc.vector.tensor_scalar_mul(w_rot[:, 0:HALF], w_sb[:, HALF:D], -1.0)
        nc.vector.tensor_copy(w_rot[:, HALF:D], w_sb[:, 0:HALF])

        def project(weights, first, count, name):
            product = psum.tile([D, count], F32, name=name)
            picked = x_sb[:].indirect(offsets[:, first // 16 : (first + count) // 16])
            nc.tensor.matmul(product[:], weights, picked, start=True, stop=True)
            return product

        for piece in range(PIECES):
            chunks = (piece * PIECE, piece * PIECE + CHUNK)
            key = project(w_sb[:, 0:D], piece * PIECE, PIECE, "key")
            if piece < PIECES - 1:
                partner = project(w_rot[:], piece * PIECE, PIECE, "partner")
                val = project(w_sb[:, D : 2 * D], piece * PIECE, PIECE, "val")
                partners = [partner[:, 0:CHUNK], partner[:, CHUNK:PIECE]]
                vals = [val[:, 0:CHUNK], val[:, CHUNK:PIECE]]
            else:
                partners = [project(w_rot[:], first, CHUNK, "partner")[:] for first in chunks]
                vals = [project(w_sb[:, D : 2 * D], first, CHUNK, "val")[:] for first in chunks]
            key_cos = work.tile([D, PIECE], F32, name="key_cos")
            nc.vector.tensor_tensor(key_cos[:], key[:], cos_sb[:, piece * PIECE : (piece + 1) * PIECE], MULT)

            for first, partner, val in zip(chunks, partners, vals):
                cols = slice(first, first + CHUNK)
                in_piece = slice(first - piece * PIECE, first - piece * PIECE + CHUNK)
                partner_sin = work.tile([D, CHUNK], F32, name="partner_sin")
                nc.vector.tensor_tensor(partner_sin[:], partner, sin_sb[:, cols], MULT)
                adder = nc.gpsimd if piece == 0 else nc.vector
                rotated = work.tile([D, CHUNK], F32, name="rotated")
                adder.tensor_tensor(rotated[:], key_cos[:, in_piece], partner_sin[:], ADD)
                nc.sync.dma_start(out[0:D, cols], rotated[:])

                val_sb = work.tile([D, CHUNK], F32, name="val_sb")
                nc.scalar.copy(val_sb[:], val)
                nc.scalar.dma_start(out[D : 2 * D, cols], val_sb[:])
